import numpy as np
import ml_dtypes


def mxq(x, axis, fmt="e4m3"):
    dtype, down = {"e4m3": (ml_dtypes.float8_e4m3fn, 7), "e5m2": (ml_dtypes.float8_e5m2, 14)}[fmt]
    v = np.moveaxis(np.asarray(x, np.float32).astype(ml_dtypes.bfloat16).astype(np.float64), axis, -1)
    blocks = v.reshape(v.shape[:-1] + (-1, 32))
    amax = np.abs(blocks).max(-1, keepdims=True)
    byte = np.maximum(np.where(amax > 0, np.frexp(amax)[1] - 1 + 127, 0) - down, 1)
    scale = np.exp2(byte - 127.0)
    codes = (blocks / scale).astype(np.float32).astype(dtype).astype(np.float64)
    return np.moveaxis((codes * scale).reshape(v.shape), -1, axis)


WIDE = False


def mx_kscale(k):
    if not WIDE:
        return np.ones(k)
    levels = np.array([20, -20, 10, -10, 0])
    a = np.random.permutation(np.resize(levels, k // 512 * 4)).reshape(k // 512, 4)
    idx = np.arange(k)
    return np.exp2(a[idx // 512, idx % 128 // 32])


BF16 = ml_dtypes.bfloat16


def bf(x):
    return np.asarray(x, np.float32).astype(BF16)


def f64(x):
    return np.asarray(x).astype(np.float64)


B, NH, T, D, N = 1, 1, 128, 16384, 512
THETA = 2.0 ** 16
SCALE = N ** -0.5


def rope_tables():
    pair = np.repeat(np.arange(N // 2), 2)
    freqs = 1.0 / THETA ** (pair * 2.0 / N)
    angles = np.arange(T)[:, None] * freqs[None, :]
    return np.cos(angles), np.sin(angles)


def rope(v, cos, sin):
    v_rot = np.stack([-v[..., 1::2], v[..., ::2]], axis=-1).reshape(v.shape)
    return v * cos + v_rot * sin


def rope_adjoint(h, cos, sin):
    hs = h * sin
    hs_rot = np.stack([hs[..., 1::2], -hs[..., ::2]], axis=-1).reshape(h.shape)
    return h * cos + hs_rot


def setup_inputs():
    u = mx_kscale(D)
    cos, sin = rope_tables()
    Q = np.random.uniform(size=(B, NH, T, N)) * 1.2 / N ** 0.25
    V = np.random.standard_normal((B, 1, T, D)) * 45.0 / np.sqrt(T) / u
    state = np.random.standard_normal((B, NH, N, D)) * 60.0 / N ** 0.75 / u
    g = np.random.standard_normal((B, NH, N, D)) * np.exp2(np.random.randint(-12, 1, (B, NH, N, 1))) * 32.0 * u
    return {"Q": bf(Q), "V": bf(V), "state": bf(state), "cos": bf(cos), "sin": bf(sin), "grad_out": bf(g)}


def reference(Q, V, state, cos, sin, grad_out):
    gQR = (mxq(f64(V), 3, "e4m3") @ np.swapaxes(mxq(f64(grad_out), 3, "e5m2"), -2, -1)) * SCALE
    return rope_adjoint(gQR, f64(cos), f64(sin))

@@ -1,0 +1,158 @@
+from contextlib import ExitStack
+
+import concourse.mybir as mybir
+from concourse.masks import make_identity
+
+F32 = mybir.dt.float32
+BF16 = mybir.dt.bfloat16
+U32 = mybir.dt.uint32
+U8 = mybir.dt.uint8
+E4M3_X4 = mybir.dt.float8_e4m3fn_x4
+E5M2_X4 = mybir.dt.float8_e5m2_x4
+MULT = mybir.AluOpType.mult
+ADD = mybir.AluOpType.add
+
+P = 128
+TOKENS = 128
+FEATURES = 512
+K_TOTAL = 16384
+SCALE = FEATURES ** -0.5
+
+PACK = 4
+K_PASS = P * PACK
+HALVES = 2
+PASSES_PER_SLAB = 4
+K_SLAB = PASSES_PER_SLAB * K_PASS
+CHUNKS = K_TOTAL // K_SLAB
+FEATURE_GROUPS = FEATURES // P
+SLABS_PER_CHUNK = 1 + FEATURE_GROUPS
+PASSES_PER_BANK = 2
+BANKS_PER_SLAB = PASSES_PER_SLAB // PASSES_PER_BANK
+WORDS_PER_BANK = PASSES_PER_BANK * HALVES * P
+
+FLOPS = 2 * TOKENS * FEATURES * K_TOTAL
+BYTES = 2 * (TOKENS + FEATURES) * K_TOTAL + 2 * 2 * TOKENS * FEATURES + 4 * TOKENS * FEATURES
+
+
+def transpose_slab(nc, banks, identity, slab, grouped, copy_out):
+    slab_words = slab[:].bitcast(F32)
+    grouped_words = grouped[:].bitcast(F32)
+    for b in range(BANKS_PER_SLAB):
+        bank = banks.tile([P, PASSES_PER_BANK, HALVES, P], F32, name="bank")
+        for j in range(PASSES_PER_BANK):
+            for u in range(HALVES):
+                first_word = ((b * PASSES_PER_BANK + j) * HALVES + u) * P
+                nc.tensor.transpose(bank[:, j, u, :], slab_words[:, first_word : first_word + P], identity[:])
+        copy_out(
+            out=grouped_words[:, b * WORDS_PER_BANK : (b + 1) * WORDS_PER_BANK].rearrange(
+                "p (j row u) -> p j row u", j=PASSES_PER_BANK, u=HALVES
+            ),
+            in_=bank[:].rearrange("p j u row -> p j row u"),
+        )
+
+
+def tile_attention_pb_k_kernel(tc, Q, V, state, cos, sin, grad_out, out):
+    nc = tc.nc
+    v_rows = V[0, 0]
+    g_rows = grad_out[0, 0]
+
+    with ExitStack() as ctx:
+        ctx.enter_context(tc.manual_schedule())
+        constants = ctx.enter_context(tc.tile_pool(name="constants", bufs=1))
+        resident = ctx.enter_context(tc.tile_pool(name="resident", bufs=1))
+        staging = ctx.enter_context(tc.tile_pool(name="staging", bufs=3))
+        operands = ctx.enter_context(tc.tile_pool(name="operands", bufs=2))
+        epilogue = ctx.enter_context(tc.tile_pool(name="epilogue", bufs=1))
+        banks = ctx.enter_context(tc.psum_pool(name="banks", bufs=7))
+        sums = ctx.enter_context(tc.psum_pool(name="sums", bufs=1))
+
+        identity = constants.tile([P, P], F32)
+        make_identity(nc, identity[:])
+
+        cos_sb = constants.tile([P, FEATURES], BF16)
+        sin_sb = constants.tile([P, FEATURES], BF16)
+        slabs = {}
+        for c in range(CHUNKS):
+            k_cols = slice(c * K_SLAB, (c + 1) * K_SLAB)
+            for s in range(SLABS_PER_CHUNK):
+                slab = resident.tile([P, K_SLAB], BF16, name="slab_%d_%d" % (c, s))
+                if s == 0:
+                    nc.sync.dma_start(out=slab[:], in_=v_rows[:, k_cols])
+                else:
+                    nc.sync.dma_start(out=slab[:], in_=g_rows[(s - 1) * P : s * P, k_cols])
+                slabs[(c, s)] = slab
+            if c == 0:
+                nc.sync.dma_start(out=cos_sb[:], in_=cos)
+                nc.sync.dma_start(out=sin_sb[:], in_=sin)
+
+        h_sum = sums.tile([P, FEATURES], F32)
+
+        def quantise_slab(s, grouped, chunk_operands):
+            v_codes, v_scales, g_codes, g_scales = chunk_operands
+            if s == 0:
+                nc.vector.quantize_mx(out=v_codes[:].bitcast(E4M3_X4), scales=v_scales[:], in_=grouped[:])
+            else:
+                rows = slice((s - 1) * P, s * P)
+                for j in range(PASSES_PER_SLAB):
+                    nc.vector.quantize_mx(
+                        out=g_codes[:, j, rows].bitcast(E5M2_X4),
+                        scales=g_scales[:, j, rows],
+                        in_=grouped[:, j * K_PASS : (j + 1) * K_PASS],
+                    )
+
+        def multiply_chunk(c, chunk_operands):
+            v_codes, v_scales, g_codes, g_scales = chunk_operands
+            for j in range(PASSES_PER_SLAB):
+                tokens = slice(j * TOKENS, (j + 1) * TOKENS)
+                nc.tensor.matmul_mx(
+                    out=h_sum[:],
+                    lhsT=v_codes[:, tokens].bitcast(E4M3_X4),
+                    lhsT_scale=v_scales[:, tokens],
+                    rhs=g_codes[:, j, :].bitcast(E5M2_X4),
+                    rhs_scale=g_scales[:, j, :],
+                    start=(c == 0 and j == 0),
+                    stop=(c == CHUNKS - 1 and j == PASSES_PER_SLAB - 1),
+                )
+
+        previous = None
+        operands_of = {}
+        for c in range(CHUNKS):
+            operands_of[c] = (
+                operands.tile([P, PASSES_PER_SLAB * TOKENS], U32, name="v_codes", align_bytes=64),
+                operands.tile([P, PASSES_PER_SLAB * TOKENS], U8, name="v_scales", align_bytes=64),
+                operands.tile([P, PASSES_PER_SLAB, FEATURES], U32, name="g_codes", align_bytes=64),
+                operands.tile([P, PASSES_PER_SLAB, FEATURES], U8, name="g_scales", align_bytes=64),
+            )
+            for s in range(SLABS_PER_CHUNK):
+                if previous is not None:
+                    quantise_slab(*previous)
+                grouped = staging.tile([P, K_SLAB], BF16, name="grouped", align_bytes=64)
+                copy_out = nc.vector.tensor_copy if s == 0 else nc.scalar.copy
+                transpose_slab(nc, banks, identity, slabs[(c, s)], grouped, copy_out)
+                previous = (s, grouped, operands_of[c])
+                if s == 1 and c > 0:
+                    multiply_chunk(c - 1, operands_of[c - 1])
+        quantise_slab(*previous)
+        multiply_chunk(CHUNKS - 1, operands_of[CHUNKS - 1])
+
+        h_pairs = h_sum[:].rearrange("p (i two) -> p i two", two=2)
+        sin_pairs = sin_sb[:].rearrange("p (i two) -> p i two", two=2)
+        cos_term = epilogue.tile([P, FEATURES], F32)
+        sin_term = epilogue.tile([P, 2, FEATURES // 2], F32)
+        result = epilogue.tile([P, FEATURES], F32)
+        nc.vector.scalar_tensor_tensor(
+            out=cos_term[:], in0=h_sum[:], scalar=SCALE, in1=cos_sb[:], op0=MULT, op1=MULT
+        )
+        nc.vector.scalar_tensor_tensor(
+            out=sin_term[:, 0, :], in0=h_pairs[:, :, 1], scalar=SCALE, in1=sin_pairs[:, :, 1], op0=MULT, op1=MULT
+        )
+        nc.vector.scalar_tensor_tensor(
+            out=sin_term[:, 1, :], in0=h_pairs[:, :, 0], scalar=-SCALE, in1=sin_pairs[:, :, 0], op0=MULT, op1=MULT
+        )
+        nc.vector.tensor_tensor(
+            out=result[:].rearrange("p (i two) -> p i two", two=2),
+            in0=cos_term[:].rearrange("p (i two) -> p i two", two=2),
+            in1=sin_term[:].rearrange("p two i -> p i two"),
+            op=ADD,
+        )
+        nc.sync.dma_start(out=out[0, 0], in_=result[:])

@@ -24,31 +24,33 @@ HALVES = 2
 PASSES_PER_SLAB = 4
 K_SLAB = PASSES_PER_SLAB * K_PASS
 CHUNKS = K_TOTAL // K_SLAB
+PASSES = K_TOTAL // K_PASS
 FEATURE_GROUPS = FEATURES // P
 SLABS_PER_CHUNK = 1 + FEATURE_GROUPS
 PASSES_PER_BANK = 2
 BANKS_PER_SLAB = PASSES_PER_SLAB // PASSES_PER_BANK
 WORDS_PER_BANK = PASSES_PER_BANK * HALVES * P
+PASSES_PER_RUN = 2
+BANKS_PER_RUN = PASSES_PER_RUN * SLABS_PER_CHUNK * BANKS_PER_SLAB // PASSES_PER_SLAB
 
 FLOPS = 2 * TOKENS * FEATURES * K_TOTAL
 BYTES = 2 * (TOKENS + FEATURES) * K_TOTAL + 2 * 2 * TOKENS * FEATURES + 4 * TOKENS * FEATURES
 
 
-def transpose_slab(nc, banks, identity, slab, grouped, copy_out):
+def transpose_bank(nc, banks, identity, slab, grouped, b, copy_out):
     slab_words = slab[:].bitcast(F32)
     grouped_words = grouped[:].bitcast(F32)
-    for b in range(BANKS_PER_SLAB):
-        bank = banks.tile([P, PASSES_PER_BANK, HALVES, P], F32, name="bank")
-        for j in range(PASSES_PER_BANK):
-            for u in range(HALVES):
-                first_word = ((b * PASSES_PER_BANK + j) * HALVES + u) * P
-                nc.tensor.transpose(bank[:, j, u, :], slab_words[:, first_word : first_word + P], identity[:])
-        copy_out(
-            out=grouped_words[:, b * WORDS_PER_BANK : (b + 1) * WORDS_PER_BANK].rearrange(
-                "p (j row u) -> p j row u", j=PASSES_PER_BANK, u=HALVES
-            ),
-            in_=bank[:].rearrange("p j u row -> p j row u"),
-        )
+    bank = banks.tile([P, PASSES_PER_BANK, HALVES, P], F32, name="bank")
+    for j in range(PASSES_PER_BANK):
+        for u in range(HALVES):
+            first_word = ((b * PASSES_PER_BANK + j) * HALVES + u) * P
+            nc.tensor.transpose(bank[:, j, u, :], slab_words[:, first_word : first_word + P], identity[:])
+    copy_out(
+        out=grouped_words[:, b * WORDS_PER_BANK : (b + 1) * WORDS_PER_BANK].rearrange(
+            "p (j row u) -> p j row u", j=PASSES_PER_BANK, u=HALVES
+        ),
+        in_=bank[:].rearrange("p j u row -> p j row u"),
+    )
 
 
 def tile_attention_pb_k_kernel(tc, Q, V, state, cos, sin, grad_out, out):
@@ -100,9 +102,10 @@ def tile_attention_pb_k_kernel(tc, Q, V, state, cos, sin, grad_out, out):
                         in_=grouped[:, j * K_PASS : (j + 1) * K_PASS],
                     )
 
-        def multiply_chunk(c, chunk_operands):
-            v_codes, v_scales, g_codes, g_scales = chunk_operands
-            for j in range(PASSES_PER_SLAB):
+        def multiply(first_pass, end_pass):
+            for g in range(first_pass, end_pass):
+                v_codes, v_scales, g_codes, g_scales = operands_of[g // PASSES_PER_SLAB]
+                j = g % PASSES_PER_SLAB
                 tokens = slice(j * TOKENS, (j + 1) * TOKENS)
                 nc.tensor.matmul_mx(
                     out=h_sum[:],
@@ -110,12 +113,14 @@ def tile_attention_pb_k_kernel(tc, Q, V, state, cos, sin, grad_out, out):
                     lhsT_scale=v_scales[:, tokens],
                     rhs=g_codes[:, j, :].bitcast(E5M2_X4),
                     rhs_scale=g_scales[:, j, :],
-                    start=(c == 0 and j == 0),
-                    stop=(c == CHUNKS - 1 and j == PASSES_PER_SLAB - 1),
+                    start=(g == 0),
+                    stop=(g == PASSES - 1),
                 )
 
         previous = None
         operands_of = {}
+        banks_done = 0
+        passes_done = 0
         for c in range(CHUNKS):
             operands_of[c] = (
                 operands.tile([P, PASSES_PER_SLAB * TOKENS], U32, name="v_codes", align_bytes=64),
@@ -128,12 +133,15 @@ def tile_attention_pb_k_kernel(tc, Q, V, state, cos, sin, grad_out, out):
                     quantise_slab(*previous)
                 grouped = staging.tile([P, K_SLAB], BF16, name="grouped", align_bytes=64)
                 copy_out = nc.vector.tensor_copy if s == 0 else nc.scalar.copy
-                transpose_slab(nc, banks, identity, slabs[(c, s)], grouped, copy_out)
+                for b in range(BANKS_PER_SLAB):
+                    transpose_bank(nc, banks, identity, slabs[(c, s)], grouped, b, copy_out)
+                    banks_done += 1
+                    if banks_done % BANKS_PER_RUN == 0 and passes_done + PASSES_PER_RUN <= c * PASSES_PER_SLAB:
+                        multiply(passes_done, passes_done + PASSES_PER_RUN)
+                        passes_done += PASSES_PER_RUN
                 previous = (s, grouped, operands_of[c])
-                if s == 1 and c > 0:
-                    multiply_chunk(c - 1, operands_of[c - 1])
         quantise_slab(*previous)
-        multiply_chunk(CHUNKS - 1, operands_of[CHUNKS - 1])
+        multiply(passes_done, PASSES)
 
         h_pairs = h_sum[:].rearrange("p (i two) -> p i two", two=2)
         sin_pairs = sin_sb[:].rearrange("p (i two) -> p i two", two=2)

@@ -30,6 +30,7 @@ SLABS_PER_CHUNK = 1 + FEATURE_GROUPS
 PASSES_PER_BANK = 2
 BANKS_PER_SLAB = PASSES_PER_SLAB // PASSES_PER_BANK
 WORDS_PER_BANK = PASSES_PER_BANK * HALVES * P
+SHARED_SLAB = SLABS_PER_CHUNK - 2
 PASSES_PER_RUN = 2
 BANKS_PER_RUN = PASSES_PER_RUN * SLABS_PER_CHUNK * BANKS_PER_SLAB // PASSES_PER_SLAB
 
@@ -83,9 +84,8 @@ def tile_attention_pb_k_kernel(tc, Q, V, state, cos, sin, grad_out, out):
                 else:
                     nc.sync.dma_start(out=slab[:], in_=g_rows[(s - 1) * P : s * P, k_cols])
                 slabs[(c, s)] = slab
-            if c == 0:
-                nc.sync.dma_start(out=cos_sb[:], in_=cos)
-                nc.sync.dma_start(out=sin_sb[:], in_=sin)
+        nc.sync.dma_start(out=cos_sb[:], in_=cos)
+        nc.sync.dma_start(out=sin_sb[:], in_=sin)
 
         h_sum = sums.tile([P, FEATURES], F32)
 
@@ -132,8 +132,9 @@ def tile_attention_pb_k_kernel(tc, Q, V, state, cos, sin, grad_out, out):
                 if previous is not None:
                     quantise_slab(*previous)
                 grouped = staging.tile([P, K_SLAB], BF16, name="grouped", align_bytes=64)
-                copy_out = nc.vector.tensor_copy if s == 0 else nc.scalar.copy
                 for b in range(BANKS_PER_SLAB):
+                    on_vector = s == 0 or (s == SHARED_SLAB and b == BANKS_PER_SLAB - 1)
+                    copy_out = nc.vector.tensor_copy if on_vector else nc.scalar.copy
                     transpose_bank(nc, banks, identity, slabs[(c, s)], grouped, b, copy_out)
                     banks_done += 1
                     if banks_done % BANKS_PER_RUN == 0 and passes_done + PASSES_PER_RUN <= c * PASSES_PER_SLAB:

@@ -21,37 +21,22 @@ SCALE = FEATURES ** -0.5
 PACK = 4
 K_PASS = P * PACK
 HALVES = 2
-PASSES_PER_SLAB = 4
-K_SLAB = PASSES_PER_SLAB * K_PASS
-CHUNKS = K_TOTAL // K_SLAB
 PASSES = K_TOTAL // K_PASS
 FEATURE_GROUPS = FEATURES // P
 SLABS_PER_CHUNK = 1 + FEATURE_GROUPS
 PASSES_PER_BANK = 2
-BANKS_PER_SLAB = PASSES_PER_SLAB // PASSES_PER_BANK
-WORDS_PER_BANK = PASSES_PER_BANK * HALVES * P
+WORDS_PER_PASS = HALVES * P
+
+CHUNK_PASSES = (4, 4, 4, 4, 4, 4, 4, 4)
+LAST_SLAB_PIECES = (1, 1, 1, 1)
 SHARED_SLAB = SLABS_PER_CHUNK - 2
+QUANTISE_LAG = 2
 PASSES_PER_RUN = 2
-BANKS_PER_RUN = PASSES_PER_RUN * SLABS_PER_CHUNK * BANKS_PER_SLAB // PASSES_PER_SLAB
+RUN_DELAY = 2
+RUN_SPACING = 4
 
 FLOPS = 2 * TOKENS * FEATURES * K_TOTAL
 BYTES = 2 * (TOKENS + FEATURES) * K_TOTAL + 2 * 2 * TOKENS * FEATURES + 4 * TOKENS * FEATURES
-
-
-def transpose_bank(nc, banks, identity, slab, grouped, b, copy_out):
-    slab_words = slab[:].bitcast(F32)
-    grouped_words = grouped[:].bitcast(F32)
-    bank = banks.tile([P, PASSES_PER_BANK, HALVES, P], F32, name="bank")
-    for j in range(PASSES_PER_BANK):
-        for u in range(HALVES):
-            first_word = ((b * PASSES_PER_BANK + j) * HALVES + u) * P
-            nc.tensor.transpose(bank[:, j, u, :], slab_words[:, first_word : first_word + P], identity[:])
-    copy_out(
-        out=grouped_words[:, b * WORDS_PER_BANK : (b + 1) * WORDS_PER_BANK].rearrange(
-            "p (j row u) -> p j row u", j=PASSES_PER_BANK, u=HALVES
-        ),
-        in_=bank[:].rearrange("p j u row -> p j row u"),
-    )
 
 
 def tile_attention_pb_k_kernel(tc, Q, V, state, cos, sin, grad_out, out):
@@ -63,7 +48,7 @@ def tile_attention_pb_k_kernel(tc, Q, V, state, cos, sin, grad_out, out):
         ctx.enter_context(tc.manual_schedule())
         constants = ctx.enter_context(tc.tile_pool(name="constants", bufs=1))
         resident = ctx.enter_context(tc.tile_pool(name="resident", bufs=1))
-        staging = ctx.enter_context(tc.tile_pool(name="staging", bufs=3))
+        staging = ctx.enter_context(tc.tile_pool(name="staging", bufs=6))
         operands = ctx.enter_context(tc.tile_pool(name="operands", bufs=2))
         epilogue = ctx.enter_context(tc.tile_pool(name="epilogue", bufs=1))
         banks = ctx.enter_context(tc.psum_pool(name="banks", bufs=7))
@@ -74,38 +59,79 @@ def tile_attention_pb_k_kernel(tc, Q, V, state, cos, sin, grad_out, out):
 
         cos_sb = constants.tile([P, FEATURES], BF16)
         sin_sb = constants.tile([P, FEATURES], BF16)
-        slabs = {}
-        for c in range(CHUNKS):
-            k_cols = slice(c * K_SLAB, (c + 1) * K_SLAB)
+        units = []
+        chunk_of_pass = []
+        first_pass_of_chunk = []
+        units_of_chunk = []
+        for c, width in enumerate(CHUNK_PASSES):
+            first_pass = len(chunk_of_pass)
+            first_pass_of_chunk.append(first_pass)
+            chunk_of_pass.extend([c] * width)
+            units_before = len(units)
             for s in range(SLABS_PER_CHUNK):
-                slab = resident.tile([P, K_SLAB], BF16, name="slab_%d_%d" % (c, s))
-                if s == 0:
-                    nc.sync.dma_start(out=slab[:], in_=v_rows[:, k_cols])
-                else:
-                    nc.sync.dma_start(out=slab[:], in_=g_rows[(s - 1) * P : s * P, k_cols])
-                slabs[(c, s)] = slab
+                very_last = c == len(CHUNK_PASSES) - 1 and s == SLABS_PER_CHUNK - 1
+                j0 = 0
+                for n in LAST_SLAB_PIECES if very_last else (width,):
+                    piece = resident.tile([P, n * K_PASS], BF16, name="piece_%d_%d_%d" % (c, s, j0))
+                    k_cols = slice((first_pass + j0) * K_PASS, (first_pass + j0 + n) * K_PASS)
+                    if s == 0:
+                        nc.sync.dma_start(out=piece[:], in_=v_rows[:, k_cols])
+                    else:
+                        nc.sync.dma_start(out=piece[:], in_=g_rows[(s - 1) * P : s * P, k_cols])
+                    for b in range(0, n, PASSES_PER_BANK):
+                        units.append((c, s, piece, b, j0 + b, min(PASSES_PER_BANK, n - b), j0 + b + PASSES_PER_BANK >= width))
+                    j0 += n
+            units_of_chunk.append(len(units) - units_before)
+        assert len(chunk_of_pass) == PASSES
         nc.sync.dma_start(out=cos_sb[:], in_=cos)
         nc.sync.dma_start(out=sin_sb[:], in_=sin)
 
         h_sum = sums.tile([P, FEATURES], F32)
+        operands_of = {}
+        grouped_of = {}
 
-        def quantise_slab(s, grouped, chunk_operands):
-            v_codes, v_scales, g_codes, g_scales = chunk_operands
+        def transpose_unit(i):
+            c, s, piece, b, j0, n, last_of_slab = units[i]
+            piece_words = piece[:].bitcast(F32)
+            bank = banks.tile([P, PASSES_PER_BANK, HALVES, P], F32, name="bank")
+            for j in range(n):
+                for u in range(HALVES):
+                    first_word = ((b + j) * HALVES + u) * P
+                    nc.tensor.transpose(bank[:, j, u, :], piece_words[:, first_word : first_word + P], identity[:])
+            grouped = staging.tile([P, PASSES_PER_BANK * K_PASS], BF16, name="grouped", align_bytes=64)
+            grouped_of[i] = grouped
+            on_vector = s == 0 or (s == SHARED_SLAB and last_of_slab and CHUNK_PASSES[c] > PASSES_PER_BANK)
+            copy_out = nc.vector.tensor_copy if on_vector else nc.scalar.copy
+            copy_out(
+                out=grouped[:].bitcast(F32)[:, : n * WORDS_PER_PASS].rearrange(
+                    "p (j row u) -> p j row u", j=n, u=HALVES
+                ),
+                in_=bank[:, 0:n].rearrange("p j u row -> p j row u"),
+            )
+
+        def quantise_unit(i):
+            c, s, piece, b, j0, n, last_of_slab = units[i]
+            v_codes, v_scales, g_codes, g_scales = operands_of[c]
+            grouped = grouped_of[i]
             if s == 0:
-                nc.vector.quantize_mx(out=v_codes[:].bitcast(E4M3_X4), scales=v_scales[:], in_=grouped[:])
+                tokens = slice(j0 * TOKENS, (j0 + n) * TOKENS)
+                nc.vector.quantize_mx(
+                    out=v_codes[:, tokens].bitcast(E4M3_X4), scales=v_scales[:, tokens], in_=grouped[:, : n * K_PASS]
+                )
             else:
                 rows = slice((s - 1) * P, s * P)
-                for j in range(PASSES_PER_SLAB):
+                for j in range(n):
                     nc.vector.quantize_mx(
-                        out=g_codes[:, j, rows].bitcast(E5M2_X4),
-                        scales=g_scales[:, j, rows],
+                        out=g_codes[:, j0 + j, rows].bitcast(E5M2_X4),
+                        scales=g_scales[:, j0 + j, rows],
                         in_=grouped[:, j * K_PASS : (j + 1) * K_PASS],
                     )
 
         def multiply(first_pass, end_pass):
             for g in range(first_pass, end_pass):
-                v_codes, v_scales, g_codes, g_scales = operands_of[g // PASSES_PER_SLAB]
-                j = g % PASSES_PER_SLAB
+                c = chunk_of_pass[g]
+                v_codes, v_scales, g_codes, g_scales = operands_of[c]
+                j = g - first_pass_of_chunk[c]
                 tokens = slice(j * TOKENS, (j + 1) * TOKENS)
                 nc.tensor.matmul_mx(
                     out=h_sum[:],
@@ -117,31 +143,35 @@ def tile_attention_pb_k_kernel(tc, Q, V, state, cos, sin, grad_out, out):
                     stop=(g == PASSES - 1),
                 )
 
-        previous = None
-        operands_of = {}
-        banks_done = 0
+        quantised_in_chunk = [0] * len(CHUNK_PASSES)
+        ready_at = {}
         passes_done = 0
-        for c in range(CHUNKS):
-            operands_of[c] = (
-                operands.tile([P, PASSES_PER_SLAB * TOKENS], U32, name="v_codes", align_bytes=64),
-                operands.tile([P, PASSES_PER_SLAB * TOKENS], U8, name="v_scales", align_bytes=64),
-                operands.tile([P, PASSES_PER_SLAB, FEATURES], U32, name="g_codes", align_bytes=64),
-                operands.tile([P, PASSES_PER_SLAB, FEATURES], U8, name="g_scales", align_bytes=64),
-            )
-            for s in range(SLABS_PER_CHUNK):
-                if previous is not None:
-                    quantise_slab(*previous)
-                grouped = staging.tile([P, K_SLAB], BF16, name="grouped", align_bytes=64)
-                for b in range(BANKS_PER_SLAB):
-                    on_vector = s == 0 or (s == SHARED_SLAB and b == BANKS_PER_SLAB - 1)
-                    copy_out = nc.vector.tensor_copy if on_vector else nc.scalar.copy
-                    transpose_bank(nc, banks, identity, slabs[(c, s)], grouped, b, copy_out)
-                    banks_done += 1
-                    if banks_done % BANKS_PER_RUN == 0 and passes_done + PASSES_PER_RUN <= c * PASSES_PER_SLAB:
-                        multiply(passes_done, passes_done + PASSES_PER_RUN)
-                        passes_done += PASSES_PER_RUN
-                previous = (s, grouped, operands_of[c])
-        quantise_slab(*previous)
+        last_run = -RUN_SPACING
+        for i in range(len(units)):
+            c = units[i][0]
+            if c not in operands_of:
+                width = CHUNK_PASSES[c]
+                operands_of[c] = (
+                    operands.tile([P, width * TOKENS], U32, name="v_codes", align_bytes=64),
+                    operands.tile([P, width * TOKENS], U8, name="v_scales", align_bytes=64),
+                    operands.tile([P, width, FEATURES], U32, name="g_codes", align_bytes=64),
+                    operands.tile([P, width, FEATURES], U8, name="g_scales", align_bytes=64),
+                )
+            if i >= QUANTISE_LAG:
+                quantise_unit(i - QUANTISE_LAG)
+                cq = units[i - QUANTISE_LAG][0]
+                quantised_in_chunk[cq] += 1
+                if quantised_in_chunk[cq] == units_of_chunk[cq]:
+                    ready_at[cq] = i
+            transpose_unit(i)
+            cp = chunk_of_pass[passes_done]
+            if cp in ready_at and i >= ready_at[cp] + RUN_DELAY and i >= last_run + RUN_SPACING:
+                end_pass = min(passes_done + PASSES_PER_RUN, first_pass_of_chunk[cp] + CHUNK_PASSES[cp])
+                multiply(passes_done, end_pass)
+                passes_done = end_pass
+                last_run = i
+        for i in range(len(units) - QUANTISE_LAG, len(units)):
+            quantise_unit(i)
         multiply(passes_done, PASSES)
 
         h_pairs = h_sum[:].rearrange("p (i two) -> p i two", two=2)

@@ -29,7 +29,6 @@ WORDS_PER_PASS = HALVES * P
 
 CHUNK_PASSES = (4, 4, 4, 4, 4, 4, 4, 4)
 LAST_SLAB_PIECES = (1, 1, 1, 1)
-SHARED_SLAB = SLABS_PER_CHUNK - 2
 QUANTISE_LAG = 2
 PASSES_PER_RUN = 2
 RUN_DELAY = 2
@@ -100,7 +99,7 @@ def tile_attention_pb_k_kernel(tc, Q, V, state, cos, sin, grad_out, out):
                     nc.tensor.transpose(bank[:, j, u, :], piece_words[:, first_word : first_word + P], identity[:])
             grouped = staging.tile([P, PASSES_PER_BANK * K_PASS], BF16, name="grouped", align_bytes=64)
             grouped_of[i] = grouped
-            on_vector = s == 0 or (s == SHARED_SLAB and last_of_slab and CHUNK_PASSES[c] > PASSES_PER_BANK)
+            on_vector = s == 0
             copy_out = nc.vector.tensor_copy if on_vector else nc.scalar.copy
             copy_out(
                 out=grouped[:].bitcast(F32)[:, : n * WORDS_PER_PASS].rearrange(

@@ -23,12 +23,13 @@ K_PASS = P * PACK
 HALVES = 2
 PASSES = K_TOTAL // K_PASS
 FEATURE_GROUPS = FEATURES // P
-SLABS_PER_CHUNK = 1 + FEATURE_GROUPS
+STREAMS = 1 + FEATURE_GROUPS
 PASSES_PER_BANK = 2
 WORDS_PER_PASS = HALVES * P
 
-CHUNK_PASSES = (4, 4, 4, 4, 4, 4, 4, 4)
-LAST_SLAB_PIECES = (1, 1, 1, 1)
+LOAD_ENDS = ((2, 8, 14, 20, 26, 32), (2, 8, 14, 20, 26, 32), (4, 10, 16, 22, 28, 32), (4, 10, 16, 22, 28, 32), (6, 12, 18, 24, 30, 32))
+PIECES_IN_SBUF = 12
+PASSES_IN_SBUF = 16
 QUANTISE_LAG = 2
 PASSES_PER_RUN = 2
 RUN_DELAY = 2
@@ -46,52 +47,62 @@ def tile_attention_pb_k_kernel(tc, Q, V, state, cos, sin, grad_out, out):
     with ExitStack() as ctx:
         ctx.enter_context(tc.manual_schedule())
         constants = ctx.enter_context(tc.tile_pool(name="constants", bufs=1))
-        resident = ctx.enter_context(tc.tile_pool(name="resident", bufs=1))
+        loaded = ctx.enter_context(tc.tile_pool(name="loaded", bufs=PIECES_IN_SBUF))
         staging = ctx.enter_context(tc.tile_pool(name="staging", bufs=6))
-        operands = ctx.enter_context(tc.tile_pool(name="operands", bufs=2))
+        v_operands = ctx.enter_context(tc.tile_pool(name="v_operands", bufs=PASSES_IN_SBUF // PASSES_PER_BANK))
+        g_operands = ctx.enter_context(tc.tile_pool(name="g_operands", bufs=PASSES_IN_SBUF))
         epilogue = ctx.enter_context(tc.tile_pool(name="epilogue", bufs=1))
         banks = ctx.enter_context(tc.psum_pool(name="banks", bufs=7))
         sums = ctx.enter_context(tc.psum_pool(name="sums", bufs=1))
 
         identity = constants.tile([P, P], F32)
         make_identity(nc, identity[:])
-
         cos_sb = constants.tile([P, FEATURES], BF16)
         sin_sb = constants.tile([P, FEATURES], BF16)
+
+        pieces = []
         units = []
-        chunk_of_pass = []
-        first_pass_of_chunk = []
-        units_of_chunk = []
-        for c, width in enumerate(CHUNK_PASSES):
-            first_pass = len(chunk_of_pass)
-            first_pass_of_chunk.append(first_pass)
-            chunk_of_pass.extend([c] * width)
-            units_before = len(units)
-            for s in range(SLABS_PER_CHUNK):
-                very_last = c == len(CHUNK_PASSES) - 1 and s == SLABS_PER_CHUNK - 1
-                j0 = 0
-                for n in LAST_SLAB_PIECES if very_last else (width,):
-                    piece = resident.tile([P, n * K_PASS], BF16, name="piece_%d_%d_%d" % (c, s, j0))
-                    k_cols = slice((first_pass + j0) * K_PASS, (first_pass + j0 + n) * K_PASS)
-                    if s == 0:
-                        nc.sync.dma_start(out=piece[:], in_=v_rows[:, k_cols])
-                    else:
-                        nc.sync.dma_start(out=piece[:], in_=g_rows[(s - 1) * P : s * P, k_cols])
-                    for b in range(0, n, PASSES_PER_BANK):
-                        units.append((c, s, piece, b, j0 + b, min(PASSES_PER_BANK, n - b), j0 + b + PASSES_PER_BANK >= width))
-                    j0 += n
-            units_of_chunk.append(len(units) - units_before)
-        assert len(chunk_of_pass) == PASSES
-        nc.sync.dma_start(out=cos_sb[:], in_=cos)
-        nc.sync.dma_start(out=sin_sb[:], in_=sin)
+        loads_done = [0] * STREAMS
+        reached = [0] * STREAMS
+        while min(reached) < PASSES:
+            s = reached.index(min(reached))
+            end = LOAD_ENDS[s][loads_done[s]]
+            n = end - reached[s]
+            for b in range(0, n, PASSES_PER_BANK):
+                units.append((s, len(pieces), b, reached[s] + b, min(PASSES_PER_BANK, n - b)))
+            pieces.append((s, reached[s], n))
+            loads_done[s] += 1
+            reached[s] = end
+        last_unit_of_piece = {}
+        for i, unit in enumerate(units):
+            last_unit_of_piece[unit[1]] = i
+
+        piece_tiles = {}
+
+        def load(m):
+            s, first_pass, n = pieces[m]
+            piece = loaded.tile([P, n * K_PASS], BF16, name="piece")
+            k_cols = slice(first_pass * K_PASS, (first_pass + n) * K_PASS)
+            if s == 0:
+                nc.sync.dma_start(out=piece[:], in_=v_rows[:, k_cols])
+            else:
+                nc.sync.dma_start(out=piece[:], in_=g_rows[(s - 1) * P : s * P, k_cols])
+            piece_tiles[m] = piece
+            if m == len(pieces) - 1:
+                nc.sync.dma_start(out=cos_sb[:], in_=cos)
+                nc.sync.dma_start(out=sin_sb[:], in_=sin)
+
+        for m in range(min(PIECES_IN_SBUF, len(pieces))):
+            load(m)
 
         h_sum = sums.tile([P, FEATURES], F32)
-        operands_of = {}
+        v_of = {}
+        g_of = {}
         grouped_of = {}
 
         def transpose_unit(i):
-            c, s, piece, b, j0, n, last_of_slab = units[i]
-            piece_words = piece[:].bitcast(F32)
+            s, m, b, g0, n = units[i]
+            piece_words = piece_tiles[m][:].bitcast(F32)
             bank = banks.tile([P, PASSES_PER_BANK, HALVES, P], F32, name="bank")
             for j in range(n):
                 for u in range(HALVES):
@@ -99,8 +110,7 @@ def tile_attention_pb_k_kernel(tc, Q, V, state, cos, sin, grad_out, out):
                     nc.tensor.transpose(bank[:, j, u, :], piece_words[:, first_word : first_word + P], identity[:])
             grouped = staging.tile([P, PASSES_PER_BANK * K_PASS], BF16, name="grouped", align_bytes=64)
             grouped_of[i] = grouped
-            on_vector = s == 0
-            copy_out = nc.vector.tensor_copy if on_vector else nc.scalar.copy
+            copy_out = nc.vector.tensor_copy if i % 5 == 0 else nc.scalar.copy
             copy_out(
                 out=grouped[:].bitcast(F32)[:, : n * WORDS_PER_PASS].rearrange(
                     "p (j row u) -> p j row u", j=n, u=HALVES
@@ -109,69 +119,75 @@ def tile_attention_pb_k_kernel(tc, Q, V, state, cos, sin, grad_out, out):
             )
 
         def quantise_unit(i):
-            c, s, piece, b, j0, n, last_of_slab = units[i]
-            v_codes, v_scales, g_codes, g_scales = operands_of[c]
+            s, m, b, g0, n = units[i]
             grouped = grouped_of[i]
             if s == 0:
-                tokens = slice(j0 * TOKENS, (j0 + n) * TOKENS)
+                v_codes = v_operands.tile([P, PASSES_PER_BANK * TOKENS], U32, name="v_codes", align_bytes=64)
+                v_scales = v_operands.tile([P, PASSES_PER_BANK * TOKENS], U8, name="v_scales", align_bytes=64)
+                for g in range(g0, g0 + n):
+                    v_of[g] = (v_codes, v_scales, g - g0)
                 nc.vector.quantize_mx(
-                    out=v_codes[:, tokens].bitcast(E4M3_X4), scales=v_scales[:, tokens], in_=grouped[:, : n * K_PASS]
+                    out=v_codes[:, : n * TOKENS].bitcast(E4M3_X4),
+                    scales=v_scales[:, : n * TOKENS],
+                    in_=grouped[:, : n * K_PASS],
                 )
             else:
                 rows = slice((s - 1) * P, s * P)
                 for j in range(n):
+                    if g0 + j not in g_of:
+                        assert len(g_of) == g0 + j and passes_done[0] > g0 + j - PASSES_IN_SBUF
+                        g_codes = g_operands.tile([P, FEATURES], U32, name="g_codes", align_bytes=64)
+                        g_scales = g_operands.tile([P, FEATURES], U8, name="g_scales", align_bytes=64)
+                        g_of[g0 + j] = (g_codes, g_scales)
+                    g_codes, g_scales = g_of[g0 + j]
                     nc.vector.quantize_mx(
-                        out=g_codes[:, j0 + j, rows].bitcast(E5M2_X4),
-                        scales=g_scales[:, j0 + j, rows],
+                        out=g_codes[:, rows].bitcast(E5M2_X4),
+                        scales=g_scales[:, rows],
                         in_=grouped[:, j * K_PASS : (j + 1) * K_PASS],
                     )
 
         def multiply(first_pass, end_pass):
             for g in range(first_pass, end_pass):
-                c = chunk_of_pass[g]
-                v_codes, v_scales, g_codes, g_scales = operands_of[c]
-                j = g - first_pass_of_chunk[c]
+                v_codes, v_scales, j = v_of[g]
+                g_codes, g_scales = g_of[g]
                 tokens = slice(j * TOKENS, (j + 1) * TOKENS)
                 nc.tensor.matmul_mx(
                     out=h_sum[:],
                     lhsT=v_codes[:, tokens].bitcast(E4M3_X4),
                     lhsT_scale=v_scales[:, tokens],
-                    rhs=g_codes[:, j, :].bitcast(E5M2_X4),
-                    rhs_scale=g_scales[:, j, :],
+                    rhs=g_codes[:].bitcast(E5M2_X4),
+                    rhs_scale=g_scales[:],
                     start=(g == 0),
                     stop=(g == PASSES - 1),
                 )
 
-        quantised_in_chunk = [0] * len(CHUNK_PASSES)
+        streams_left = [STREAMS] * PASSES
         ready_at = {}
-        passes_done = 0
+        passes_done = [0]
         last_run = -RUN_SPACING
         for i in range(len(units)):
-            c = units[i][0]
-            if c not in operands_of:
-                width = CHUNK_PASSES[c]
-                operands_of[c] = (
-                    operands.tile([P, width * TOKENS], U32, name="v_codes", align_bytes=64),
-                    operands.tile([P, width * TOKENS], U8, name="v_scales", align_bytes=64),
-                    operands.tile([P, width, FEATURES], U32, name="g_codes", align_bytes=64),
-                    operands.tile([P, width, FEATURES], U8, name="g_scales", align_bytes=64),
-                )
+            s, m, b, g0, n = units[i]
             if i >= QUANTISE_LAG:
                 quantise_unit(i - QUANTISE_LAG)
-                cq = units[i - QUANTISE_LAG][0]
-                quantised_in_chunk[cq] += 1
-                if quantised_in_chunk[cq] == units_of_chunk[cq]:
-                    ready_at[cq] = i
+                sq, mq, bq, gq, nq = units[i - QUANTISE_LAG]
+                for g in range(gq, gq + nq):
+                    streams_left[g] -= 1
+                    if streams_left[g] == 0:
+                        ready_at[g] = i
             transpose_unit(i)
-            cp = chunk_of_pass[passes_done]
-            if cp in ready_at and i >= ready_at[cp] + RUN_DELAY and i >= last_run + RUN_SPACING:
-                end_pass = min(passes_done + PASSES_PER_RUN, first_pass_of_chunk[cp] + CHUNK_PASSES[cp])
-                multiply(passes_done, end_pass)
-                passes_done = end_pass
+            if last_unit_of_piece[m] == i and m + PIECES_IN_SBUF < len(pieces):
+                load(m + PIECES_IN_SBUF)
+            due = 0
+            while passes_done[0] + due in ready_at and ready_at[passes_done[0] + due] + RUN_DELAY <= i:
+                due += 1
+            spacing = RUN_SPACING if due <= 2 * PASSES_PER_RUN else RUN_SPACING // 2
+            if due >= PASSES_PER_RUN and i >= last_run + spacing and i < len(units) - 6:
+                multiply(passes_done[0], passes_done[0] + PASSES_PER_RUN)
+                passes_done[0] += PASSES_PER_RUN
                 last_run = i
         for i in range(len(units) - QUANTISE_LAG, len(units)):
             quantise_unit(i)
-        multiply(passes_done, PASSES)
+        multiply(passes_done[0], PASSES)
 
         h_pairs = h_sum[:].rearrange("p (i two) -> p i two", two=2)
         sin_pairs = sin_sb[:].rearrange("p (i two) -> p i two", two=2)

@@ -45,7 +45,6 @@ def tile_attention_pb_k_kernel(tc, Q, V, state, cos, sin, grad_out, out):
     g_rows = grad_out[0, 0]
 
     with ExitStack() as ctx:
-        ctx.enter_context(tc.manual_schedule())
         constants = ctx.enter_context(tc.tile_pool(name="constants", bufs=1))
         loaded = ctx.enter_context(tc.tile_pool(name="loaded", bufs=PIECES_IN_SBUF))
         staging = ctx.enter_context(tc.tile_pool(name="staging", bufs=6))

from contextlib import ExitStack

import concourse.mybir as mybir
from concourse.masks import make_identity

F32 = mybir.dt.float32
BF16 = mybir.dt.bfloat16
U32 = mybir.dt.uint32
U8 = mybir.dt.uint8
E4M3_X4 = mybir.dt.float8_e4m3fn_x4
E5M2_X4 = mybir.dt.float8_e5m2_x4
MULT = mybir.AluOpType.mult
ADD = mybir.AluOpType.add

P = 128
TOKENS = 128
FEATURES = 512
K_TOTAL = 16384
SCALE = FEATURES ** -0.5

PACK = 4
K_PASS = P * PACK
HALVES = 2
PASSES = K_TOTAL // K_PASS
FEATURE_GROUPS = FEATURES // P
STREAMS = 1 + FEATURE_GROUPS
PASSES_PER_BANK = 2
WORDS_PER_PASS = HALVES * P

LOAD_ENDS = ((2, 8, 14, 20, 26, 32), (2, 8, 14, 20, 26, 32), (4, 10, 16, 22, 28, 32), (4, 10, 16, 22, 28, 32), (6, 12, 18, 24, 30, 32))
PIECES_IN_SBUF = 12
PASSES_IN_SBUF = 16
QUANTISE_LAG = 2
PASSES_PER_RUN = 2
RUN_DELAY = 2
RUN_SPACING = 4

FLOPS = 2 * TOKENS * FEATURES * K_TOTAL
BYTES = 2 * (TOKENS + FEATURES) * K_TOTAL + 2 * 2 * TOKENS * FEATURES + 4 * TOKENS * FEATURES


def tile_attention_pb_k_kernel(tc, Q, V, state, cos, sin, grad_out, out):
    nc = tc.nc
    v_rows = V[0, 0]
    g_rows = grad_out[0, 0]

    with ExitStack() as ctx:
        constants = ctx.enter_context(tc.tile_pool(name="constants", bufs=1))
        loaded = ctx.enter_context(tc.tile_pool(name="loaded", bufs=PIECES_IN_SBUF))
        staging = ctx.enter_context(tc.tile_pool(name="staging", bufs=6))
        v_operands = ctx.enter_context(tc.tile_pool(name="v_operands", bufs=PASSES_IN_SBUF // PASSES_PER_BANK))
        g_operands = ctx.enter_context(tc.tile_pool(name="g_operands", bufs=PASSES_IN_SBUF))
        epilogue = ctx.enter_context(tc.tile_pool(name="epilogue", bufs=1))
        banks = ctx.enter_context(tc.psum_pool(name="banks", bufs=7))
        sums = ctx.enter_context(tc.psum_pool(name="sums", bufs=1))

        identity = constants.tile([P, P], F32)
        make_identity(nc, identity[:])
        cos_sb = constants.tile([P, FEATURES], BF16)
        sin_sb = constants.tile([P, FEATURES], BF16)

        pieces = []
        units = []
        loads_done = [0] * STREAMS
        reached = [0] * STREAMS
        while min(reached) < PASSES:
            s = reached.index(min(reached))
            end = LOAD_ENDS[s][loads_done[s]]
            n = end - reached[s]
            for b in range(0, n, PASSES_PER_BANK):
                units.append((s, len(pieces), b, reached[s] + b, min(PASSES_PER_BANK, n - b)))
            pieces.append((s, reached[s], n))
            loads_done[s] += 1
            reached[s] = end
        last_unit_of_piece = {}
        for i, unit in enumerate(units):
            last_unit_of_piece[unit[1]] = i

        piece_tiles = {}

        def load(m):
            s, first_pass, n = pieces[m]
            piece = loaded.tile([P, n * K_PASS], BF16, name="piece")
            k_cols = slice(first_pass * K_PASS, (first_pass + n) * K_PASS)
            if s == 0:
                nc.sync.dma_start(out=piece[:], in_=v_rows[:, k_cols])
            else:
                nc.sync.dma_start(out=piece[:], in_=g_rows[(s - 1) * P : s * P, k_cols])
            piece_tiles[m] = piece
            if m == len(pieces) - 1:
                nc.sync.dma_start(out=cos_sb[:], in_=cos)
                nc.sync.dma_start(out=sin_sb[:], in_=sin)

        for m in range(min(PIECES_IN_SBUF, len(pieces))):
            load(m)

        h_sum = sums.tile([P, FEATURES], F32)
        v_of = {}
        g_of = {}
        grouped_of = {}

        def transpose_unit(i):
            s, m, b, g0, n = units[i]
            piece_words = piece_tiles[m][:].bitcast(F32)
            bank = banks.tile([P, PASSES_PER_BANK, HALVES, P], F32, name="bank")
            for j in range(n):
                for u in range(HALVES):
                    first_word = ((b + j) * HALVES + u) * P
                    nc.tensor.transpose(bank[:, j, u, :], piece_words[:, first_word : first_word + P], identity[:])
            grouped = staging.tile([P, PASSES_PER_BANK * K_PASS], BF16, name="grouped", align_bytes=64)
            grouped_of[i] = grouped
            copy_out = nc.vector.tensor_copy if i % 5 == 0 else nc.scalar.copy
            copy_out(
                out=grouped[:].bitcast(F32)[:, : n * WORDS_PER_PASS].rearrange(
                    "p (j row u) -> p j row u", j=n, u=HALVES
                ),
                in_=bank[:, 0:n].rearrange("p j u row -> p j row u"),
            )

        def quantise_unit(i):
            s, m, b, g0, n = units[i]
            grouped = grouped_of[i]
            if s == 0:
                v_codes = v_operands.tile([P, PASSES_PER_BANK * TOKENS], U32, name="v_codes", align_bytes=64)
                v_scales = v_operands.tile([P, PASSES_PER_BANK * TOKENS], U8, name="v_scales", align_bytes=64)
                for g in range(g0, g0 + n):
                    v_of[g] = (v_codes, v_scales, g - g0)
                nc.vector.quantize_mx(
                    out=v_codes[:, : n * TOKENS].bitcast(E4M3_X4),
                    scales=v_scales[:, : n * TOKENS],
                    in_=grouped[:, : n * K_PASS],
                )
            else:
                rows = slice((s - 1) * P, s * P)
                for j in range(n):
                    if g0 + j not in g_of:
                        assert len(g_of) == g0 + j and passes_done[0] > g0 + j - PASSES_IN_SBUF
                        g_codes = g_operands.tile([P, FEATURES], U32, name="g_codes", align_bytes=64)
                        g_scales = g_operands.tile([P, FEATURES], U8, name="g_scales", align_bytes=64)
                        g_of[g0 + j] = (g_codes, g_scales)
                    g_codes, g_scales = g_of[g0 + j]
                    nc.vector.quantize_mx(
                        out=g_codes[:, rows].bitcast(E5M2_X4),
                        scales=g_scales[:, rows],
                        in_=grouped[:, j * K_PASS : (j + 1) * K_PASS],
                    )

        def multiply(first_pass, end_pass):
            for g in range(first_pass, end_pass):
                v_codes, v_scales, j = v_of[g]
                g_codes, g_scales = g_of[g]
                tokens = slice(j * TOKENS, (j + 1) * TOKENS)
                nc.tensor.matmul_mx(
                    out=h_sum[:],
                    lhsT=v_codes[:, tokens].bitcast(E4M3_X4),
                    lhsT_scale=v_scales[:, tokens],
                    rhs=g_codes[:].bitcast(E5M2_X4),
                    rhs_scale=g_scales[:],
                    start=(g == 0),
                    stop=(g == PASSES - 1),
                )

        streams_left = [STREAMS] * PASSES
        ready_at = {}
        passes_done = [0]
        last_run = -RUN_SPACING
        for i in range(len(units)):
            s, m, b, g0, n = units[i]
            if i >= QUANTISE_LAG:
                quantise_unit(i - QUANTISE_LAG)
                sq, mq, bq, gq, nq = units[i - QUANTISE_LAG]
                for g in range(gq, gq + nq):
                    streams_left[g] -= 1
                    if streams_left[g] == 0:
                        ready_at[g] = i
            transpose_unit(i)
            if last_unit_of_piece[m] == i and m + PIECES_IN_SBUF < len(pieces):
                load(m + PIECES_IN_SBUF)
            due = 0
            while passes_done[0] + due in ready_at and ready_at[passes_done[0] + due] + RUN_DELAY <= i:
                due += 1
            spacing = RUN_SPACING if due <= 2 * PASSES_PER_RUN else RUN_SPACING // 2
            if due >= PASSES_PER_RUN and i >= last_run + spacing and i < len(units) - 6:
                multiply(passes_done[0], passes_done[0] + PASSES_PER_RUN)
                passes_done[0] += PASSES_PER_RUN
                last_run = i
        for i in range(len(units) - QUANTISE_LAG, len(units)):
            quantise_unit(i)
        multiply(passes_done[0], PASSES)

        h_pairs = h_sum[:].rearrange("p (i two) -> p i two", two=2)
        sin_pairs = sin_sb[:].rearrange("p (i two) -> p i two", two=2)
        cos_term = epilogue.tile([P, FEATURES], F32)
        sin_term = epilogue.tile([P, 2, FEATURES // 2], F32)
        result = epilogue.tile([P, FEATURES], F32)
        nc.vector.scalar_tensor_tensor(
            out=cos_term[:], in0=h_sum[:], scalar=SCALE, in1=cos_sb[:], op0=MULT, op1=MULT
        )
        nc.vector.scalar_tensor_tensor(
            out=sin_term[:, 0, :], in0=h_pairs[:, :, 1], scalar=SCALE, in1=sin_pairs[:, :, 1], op0=MULT, op1=MULT
        )
        nc.vector.scalar_tensor_tensor(
            out=sin_term[:, 1, :], in0=h_pairs[:, :, 0], scalar=-SCALE, in1=sin_pairs[:, :, 0], op0=MULT, op1=MULT
        )
        nc.vector.tensor_tensor(
            out=result[:].rearrange("p (i two) -> p i two", two=2),
            in0=cos_term[:].rearrange("p (i two) -> p i two", two=2),
            in1=sin_term[:].rearrange("p two i -> p i two"),
            op=ADD,
        )
        nc.sync.dma_start(out=out[0, 0], in_=result[:])
